import numpy as np
import ml_dtypes


def mxq(x, axis, fmt="e4m3"):
    dtype, down = {"e4m3": (ml_dtypes.float8_e4m3fn, 7), "e5m2": (ml_dtypes.float8_e5m2, 14)}[fmt]
    v = np.moveaxis(np.asarray(x, np.float32).astype(ml_dtypes.bfloat16).astype(np.float64), axis, -1)
    blocks = v.reshape(v.shape[:-1] + (-1, 32))
    amax = np.abs(blocks).max(-1, keepdims=True)
    byte = np.maximum(np.where(amax > 0, np.frexp(amax)[1] - 1 + 127, 0) - down, 1)
    scale = np.exp2(byte - 127.0)
    codes = (blocks / scale).astype(np.float32).astype(dtype).astype(np.float64)
    return np.moveaxis((codes * scale).reshape(v.shape), -1, axis)


WIDE = False


def mx_kscale(k):
    if not WIDE:
        return np.ones(k)
    levels = np.array([10, -10, 5, -5, 0])
    a = np.random.permutation(np.resize(levels, k // 512 * 4)).reshape(k // 512, 4)
    idx = np.arange(k)
    return np.exp2(a[idx // 512, idx % 128 // 32])


BF16 = ml_dtypes.bfloat16


def bf(x):
    return np.asarray(x, np.float32).astype(BF16)


def f64(x):
    return np.asarray(x).astype(np.float64)


B, T, C_IN, HIDDEN, HEADS, OUT_DIM = 2, 1024, 1024, 1024, 8, 1024
RMS_EPS = 1.1920928955078125e-07


def silu(z):
    return z / (1.0 + np.exp(-z))


def setup_inputs():
    s, t = mx_kscale(C_IN), mx_kscale(HIDDEN)
    r = np.exp2(-12.0 * np.random.random((B, T, 1)))
    return {"x": bf(np.random.standard_normal((B, T, C_IN)) * s),
            "h_attn": bf(np.random.standard_normal((B, T, HIDDEN)) * 0.8 * r),
            "Wu": bf(np.random.standard_normal((HIDDEN, C_IN)) / np.sqrt(C_IN) / s),
            "bu": bf(np.random.standard_normal(HIDDEN) * 0.1),
            "g_norm": bf((1.0 + 0.1 * np.random.standard_normal(HIDDEN)) * t),
            "Wf": bf(np.random.standard_normal((OUT_DIM, HIDDEN)) / np.sqrt(HIDDEN) / t),
            "b_out": bf(np.random.standard_normal(OUT_DIM) * 0.1)}


def reference(x, h_attn, Wu, bu, g_norm, Wf, b_out):
    u = silu((mxq(f64(x), 2, "e4m3") @ mxq(f64(Wu), 1, "e4m3").T) + f64(bu))
    av = f64(h_attn)
    av_norm = av * (1.0 / np.sqrt(np.mean(av * av, axis=-1, keepdims=True) + RMS_EPS)) * f64(g_norm)
    uv = av_norm * u
    return (mxq(uv, 2, "e4m3") @ mxq(f64(Wf), 1, "e4m3").T) + f64(b_out)

@@ -1,0 +1,225 @@
+import concourse.mybir as mybir
+from concourse.masks import make_identity
+
+F32 = mybir.dt.float32
+BF16 = mybir.dt.bfloat16
+U32 = mybir.dt.uint32
+U8 = mybir.dt.uint8
+FP8X4 = mybir.dt.float8_e4m3fn_x4
+ACT = mybir.ActivationFunctionType
+ALU = mybir.AluOpType
+
+P = 128
+PACK = 4
+K = 1024
+PASSES = K // (P * PACK)
+TOKENS = 2048
+OUT_DIM = 1024
+GROUP = 512
+TILES = GROUP // P
+CHUNKS = TOKENS // GROUP
+RMS_EPS = 1.1920928955078125e-07
+
+FLOPS = 2 * TOKENS * K * K + 2 * TOKENS * K * OUT_DIM
+
+
+def quantise_group(nc, pools, rows, ident, codes, scales):
+    words = rows.bitcast(F32)
+    grouped = pools["grouped"].tile([P, PASSES * GROUP * PACK], BF16, name="grouped", align_bytes=64)
+    grouped_words = grouped[:].bitcast(F32).rearrange("p (g r u) -> p g r u", g=PASSES, u=2)
+    for b in range(TILES):
+        turned = pools["psum"].tile([P, PASSES, 2, P], F32, name="turned", tag="turn")
+        for g in range(PASSES):
+            for u in range(2):
+                first = b * (K // 2) + (2 * g + u) * P
+                nc.tensor.transpose(turned[:, g, u, :], words[:, first : first + P], ident)
+        nc.scalar.copy(
+            out=grouped_words[:, :, b * P : (b + 1) * P, :],
+            in_=turned[:].rearrange("p g u r -> p g r u"),
+        )
+    nc.vector.quantize_mx(out=codes.bitcast(FP8X4), scales=scales, in_=grouped[:])
+
+
+def tile_hstu_pb_kernel(tc, x, h_attn, Wu, bu, g_norm, Wf, b_out, out):
+    nc = tc.nc
+
+    x_rows = x.flatten_outer_dims().rearrange("(c p i) k -> c p (i k)", p=P, i=TILES)
+    h_rows = h_attn.flatten_outer_dims().rearrange("(c p i) k -> c p (i k)", p=P, i=TILES)
+    out_rows = out.flatten_outer_dims().rearrange("(c p i) o -> c p i o", p=P, i=TILES)
+    wu_rows = Wu.rearrange("(g u p e) k -> g p u (e k)", g=PASSES, u=2, p=P, e=2)
+    wf_rows = Wf.rearrange("(h b p) k -> h p b k", h=OUT_DIM // GROUP, b=TILES, p=P)
+
+    with tc.tile_pool(name="const", bufs=1) as const, tc.tile_pool(name="rows", bufs=4) as rows_pool, tc.tile_pool(
+        name="hrows", bufs=2
+    ) as hrows_pool, tc.tile_pool(name="grouped", bufs=2) as grouped_pool, tc.tile_pool(
+        name="xcodes", bufs=2
+    ) as xcodes_pool, tc.tile_pool(name="norm", bufs=2) as norm_pool, tc.tile_pool(
+        name="gate", bufs=2
+    ) as gate_pool, tc.tile_pool(name="silu", bufs=4) as silu_pool, tc.tile_pool(
+        name="result", bufs=3
+    ) as result_pool, tc.psum_pool(name="psum", bufs=4) as psum:
+        pools = {"grouped": grouped_pool, "psum": psum}
+
+        ident = const.tile([P, P], F32)
+        make_identity(nc, ident[:])
+        minus_half = const.tile([P, TILES], F32)
+        nc.gpsimd.memset(minus_half[:], -0.5)
+
+        def load_rows(source, pattern, **sizes):
+            rows = rows_pool.tile([P, TILES * K], BF16, name="rows")
+            nc.sync.dma_start(out=rows[:].rearrange(pattern, **sizes), in_=source)
+            return rows
+
+        def load_x(c):
+            return load_rows(x_rows[c], "p f -> p f")
+
+        def load_h(c):
+            h_sb = hrows_pool.tile([P, TILES * K], BF16, name="h_sb")
+            nc.sync.dma_start(out=h_sb[:], in_=h_rows[c])
+            return h_sb
+
+        def weight_codes(name):
+            codes = const.tile([P, PASSES * GROUP], U32, name=name + "_codes", align_bytes=64)
+            scales = const.tile([P, PASSES * GROUP], U8, name=name + "_scales", align_bytes=64)
+            return codes, scales
+
+        def quantise_x(x_sb):
+            codes = xcodes_pool.tile([P, PASSES * GROUP], U32, name="x_codes", align_bytes=64)
+            scales = xcodes_pool.tile([P, PASSES * GROUP], U8, name="x_scales", align_bytes=64)
+            quantise_group(nc, pools, x_sb[:], ident[:], codes[:], scales[:])
+            return codes, scales
+
+        def normalise(h_sb):
+            sum_sq = norm_pool.tile([P, TILES], F32, name="sum_sq")
+            for i in range(TILES):
+                squares = norm_pool.tile([P, K], BF16, name="squares")
+                nc.scalar.activation(
+                    out=squares[:],
+                    in_=h_sb[:, i * K : (i + 1) * K],
+                    func=ACT.Square,
+                    accum_out=sum_sq[:, i : i + 1],
+                )
+            mean_sq = norm_pool.tile([P, TILES], F32, name="mean_sq")
+            nc.gpsimd.tensor_scalar(
+                out=mean_sq[:], in0=sum_sq[:], scalar1=1.0 / K, scalar2=RMS_EPS, op0=ALU.mult, op1=ALU.add
+            )
+            rstd = norm_pool.tile([P, TILES], F32, name="rstd")
+            nc.gpsimd.tensor_tensor(out=rstd[:], in0=mean_sq[:], in1=minus_half[:], op=ALU.pow)
+            h_norm = norm_pool.tile([P, TILES, K], F32, name="h_norm")
+            for i in range(TILES):
+                nc.vector.tensor_scalar(
+                    out=h_norm[:, i, :].rearrange("p (q e m) -> p q e m", e=2, m=P),
+                    in0=h_sb[:, i * K : (i + 1) * K].rearrange("p (q m e) -> p q e m", m=P, e=2),
+                    scalar1=rstd[:, i : i + 1],
+                    scalar2=None,
+                    op0=ALU.mult,
+                )
+            return h_norm
+
+        def gated_half(g2, x_q, h_norm, uv_codes, uv_scales):
+            x_codes, x_scales = x_q
+            w_codes, w_scales = wu_q[g2]
+            planes = gate_pool.tile([P, PACK, GROUP], BF16, name="planes")
+            for t in range(PACK):
+                j = PACK * g2 + t
+                z = psum.tile([P, GROUP], F32, name="z", tag="mx")
+                for g in range(PASSES):
+                    m_cols = slice(g * GROUP + t * P, g * GROUP + (t + 1) * P)
+                    n_cols = slice(g * GROUP, (g + 1) * GROUP)
+                    nc.tensor.matmul_mx(
+                        out=z[:],
+                        lhsT=w_codes[:, m_cols].bitcast(FP8X4),
+                        lhsT_scale=w_scales[:, m_cols],
+                        rhs=x_codes[:, n_cols].bitcast(FP8X4),
+                        rhs_scale=x_scales[:, n_cols],
+                        start=(g == 0),
+                        stop=(g == PASSES - 1),
+                    )
+                h_turned = psum.tile([P, GROUP], F32, name="h_turned", tag="turn")
+                for i in range(TILES):
+                    nc.tensor.transpose(
+                        h_turned[:, i * P : (i + 1) * P], h_norm[:, i, j * P : (j + 1) * P], ident[:]
+                    )
+                u = silu_pool.tile([P, GROUP], F32, name="u")
+                nc.scalar.activation(out=u[:], in_=z[:], func=ACT.Silu, bias=bu_sb[:, j : j + 1], scale=1.0)
+                nc.vector.scalar_tensor_tensor(
+                    out=planes[:, t, :],
+                    in0=h_turned[:],
+                    scalar=g_sb[:, j : j + 1],
+                    in1=u[:],
+                    op0=ALU.mult,
+                    op1=ALU.mult,
+                )
+            uv_grouped = gate_pool.tile([P, GROUP, PACK], BF16, name="uv_grouped", align_bytes=64)
+            nc.vector.tensor_copy(out=uv_grouped[:], in_=planes[:].rearrange("p t r -> p r t"))
+            cols = slice(g2 * GROUP, (g2 + 1) * GROUP)
+            nc.vector.quantize_mx(
+                out=uv_codes[:, cols].bitcast(FP8X4),
+                scales=uv_scales[:, cols],
+                in_=uv_grouped[:].rearrange("p r t -> p (r t)"),
+            )
+
+        def project(c, uv_codes, uv_scales):
+            for i in range(TILES):
+                result = result_pool.tile([P, OUT_DIM], F32, name="result")
+                for h in range(OUT_DIM // GROUP):
+                    w_codes, w_scales = wf_q[h]
+                    acc = psum.tile([P, GROUP], F32, name="acc", tag="mx")
+                    for g in range(PASSES):
+                        m_cols = slice(g * GROUP + i * P, g * GROUP + (i + 1) * P)
+                        n_cols = slice(g * GROUP, (g + 1) * GROUP)
+                        nc.tensor.matmul_mx(
+                            out=acc[:],
+                            lhsT=uv_codes[:, m_cols].bitcast(FP8X4),
+                            lhsT_scale=uv_scales[:, m_cols],
+                            rhs=w_codes[:, n_cols].bitcast(FP8X4),
+                            rhs_scale=w_scales[:, n_cols],
+                            start=(g == 0),
+                            stop=(g == PASSES - 1),
+                        )
+                    o_cols = slice(h * GROUP, (h + 1) * GROUP)
+                    nc.vector.tensor_tensor(out=result[:, o_cols], in0=acc[:], in1=b_out_sb[:, o_cols], op=ALU.add)
+                nc.sync.dma_start(out=out_rows[c][:, i, :], in_=result[:])
+
+        wu_sb = [None, None]
+        wf_sb = [None, None]
+        wu_sb[0] = load_rows(wu_rows[0], "p (u f) -> p u f", u=2)
+        x_sb = load_x(0)
+        wu_sb[1] = load_rows(wu_rows[1], "p (u f) -> p u f", u=2)
+        h_sb = load_h(0)
+        bu_sb = const.tile([P, 2 * PACK], BF16)
+        nc.scalar.dma_start(
+            out=bu_sb[:].rearrange("p (q e) -> p q e", e=2), in_=bu.rearrange("(q p e) -> p q e", p=P, e=2)
+        )
+        g_sb = const.tile([P, 2 * PACK], BF16)
+        nc.scalar.dma_start(
+            out=g_sb[:].rearrange("p (q e) -> p q e", e=2), in_=g_norm.rearrange("(q p e) -> p q e", p=P, e=2)
+        )
+
+        wu_q = [weight_codes("wu0"), weight_codes("wu1")]
+        wf_q = [weight_codes("wf0"), weight_codes("wf1")]
+        quantise_group(nc, pools, wu_sb[0][:], ident[:], wu_q[0][0][:], wu_q[0][1][:])
+        x_q = quantise_x(x_sb)
+        quantise_group(nc, pools, wu_sb[1][:], ident[:], wu_q[1][0][:], wu_q[1][1][:])
+        h_norm = normalise(h_sb)
+
+        for h in range(2):
+            wf_sb[h] = load_rows(wf_rows[h], "p (b k) -> p b k", b=TILES)
+        b_out_sb = const.tile([P, OUT_DIM], BF16)
+        nc.sync.dma_start(out=b_out_sb[:], in_=b_out.partition_broadcast(P))
+
+        for c in range(CHUNKS):
+            if c + 1 < CHUNKS:
+                x_sb = load_x(c + 1)
+                h_sb = load_h(c + 1)
+            uv_codes = gate_pool.tile([P, PASSES * GROUP], U32, name="uv_codes", align_bytes=64)
+            uv_scales = gate_pool.tile([P, PASSES * GROUP], U8, name="uv_scales", align_bytes=64)
+            for g2 in range(PASSES):
+                gated_half(g2, x_q, h_norm, uv_codes, uv_scales)
+            if c == 0:
+                for h in range(2):
+                    quantise_group(nc, pools, wf_sb[h][:], ident[:], wf_q[h][0][:], wf_q[h][1][:])
+            if c + 1 < CHUNKS:
+                x_q = quantise_x(x_sb)
+                h_norm = normalise(h_sb)
+            project(c, uv_codes, uv_scales)

@@ -1,3 +1,5 @@
+from contextlib import ExitStack
+
 import concourse.mybir as mybir
 from concourse.masks import make_identity
 
@@ -18,26 +20,15 @@ OUT_DIM = 1024
 GROUP = 512
 TILES = GROUP // P
 CHUNKS = TOKENS // GROUP
+HALVES = OUT_DIM // GROUP
+TOKEN_TILES = TOKENS // P
+PAIRS = K // (2 * P)
+ROUNDS = CHUNKS * PAIRS
+AHEAD = 4
+LAG = 6
 RMS_EPS = 1.1920928955078125e-07
 
 FLOPS = 2 * TOKENS * K * K + 2 * TOKENS * K * OUT_DIM
-
-
-def quantise_group(nc, pools, rows, ident, codes, scales):
-    words = rows.bitcast(F32)
-    grouped = pools["grouped"].tile([P, PASSES * GROUP * PACK], BF16, name="grouped", align_bytes=64)
-    grouped_words = grouped[:].bitcast(F32).rearrange("p (g r u) -> p g r u", g=PASSES, u=2)
-    for b in range(TILES):
-        turned = pools["psum"].tile([P, PASSES, 2, P], F32, name="turned", tag="turn")
-        for g in range(PASSES):
-            for u in range(2):
-                first = b * (K // 2) + (2 * g + u) * P
-                nc.tensor.transpose(turned[:, g, u, :], words[:, first : first + P], ident)
-        nc.scalar.copy(
-            out=grouped_words[:, :, b * P : (b + 1) * P, :],
-            in_=turned[:].rearrange("p g u r -> p g r u"),
-        )
-    nc.vector.quantize_mx(out=codes.bitcast(FP8X4), scales=scales, in_=grouped[:])
 
 
 def tile_hstu_pb_kernel(tc, x, h_attn, Wu, bu, g_norm, Wf, b_out, out):
@@ -47,179 +38,248 @@ def tile_hstu_pb_kernel(tc, x, h_attn, Wu, bu, g_norm, Wf, b_out, out):
     h_rows = h_attn.flatten_outer_dims().rearrange("(c p i) k -> c p (i k)", p=P, i=TILES)
     out_rows = out.flatten_outer_dims().rearrange("(c p i) o -> c p i o", p=P, i=TILES)
     wu_rows = Wu.rearrange("(g u p e) k -> g p u (e k)", g=PASSES, u=2, p=P, e=2)
-    wf_rows = Wf.rearrange("(h b p) k -> h p b k", h=OUT_DIM // GROUP, b=TILES, p=P)
+    wf_rows = Wf.rearrange("(h b p) k -> h p b k", h=HALVES, b=TILES, p=P)
 
-    with tc.tile_pool(name="const", bufs=1) as const, tc.tile_pool(name="rows", bufs=4) as rows_pool, tc.tile_pool(
-        name="hrows", bufs=2
-    ) as hrows_pool, tc.tile_pool(name="grouped", bufs=2) as grouped_pool, tc.tile_pool(
-        name="xcodes", bufs=2
-    ) as xcodes_pool, tc.tile_pool(name="norm", bufs=2) as norm_pool, tc.tile_pool(
-        name="gate", bufs=2
-    ) as gate_pool, tc.tile_pool(name="silu", bufs=4) as silu_pool, tc.tile_pool(
-        name="result", bufs=3
-    ) as result_pool, tc.psum_pool(name="psum", bufs=4) as psum:
-        pools = {"grouped": grouped_pool, "psum": psum}
+    with ExitStack() as stack:
 
-        ident = const.tile([P, P], F32)
+        def open_pool(name, bufs):
+            return stack.enter_context(tc.tile_pool(name=name, bufs=bufs))
+
+        keep = open_pool("keep", 1)
+        grouped_pool = open_pool("grouped", 6)
+        x_pool = open_pool("xcodes", 2)
+        norm_pool = open_pool("norm", 2)
+        stats_pool = open_pool("stats", 4)
+        silu_pool = open_pool("silu", 4)
+        gate_pool = open_pool("gate", 2)
+        result_pool = open_pool("result", 3)
+        psum = stack.enter_context(tc.psum_pool(name="psum", bufs=2))
+        stack.enter_context(tc.manual_schedule())
+
+        ident = keep.tile([P, P], F32)
         make_identity(nc, ident[:])
-        minus_half = const.tile([P, TILES], F32)
+        minus_half = keep.tile([P, 1], F32)
         nc.gpsimd.memset(minus_half[:], -0.5)
 
-        def load_rows(source, pattern, **sizes):
-            rows = rows_pool.tile([P, TILES * K], BF16, name="rows")
+        bu_sb = keep.tile([P, 2 * PACK], BF16)
+        nc.scalar.dma_start(
+            out=bu_sb[:].rearrange("p (q e) -> p q e", e=2), in_=bu.rearrange("(q p e) -> p q e", p=P, e=2)
+        )
+        g_sb = keep.tile([P, 2 * PACK], BF16)
+        nc.scalar.dma_start(
+            out=g_sb[:].rearrange("p (q e) -> p q e", e=2), in_=g_norm.rearrange("(q p e) -> p q e", p=P, e=2)
+        )
+        table_warm = keep.tile([P, 1], F32)
+        nc.scalar.activation(out=table_warm[:], in_=minus_half[:], func=ACT.Silu)
+
+        def load(name, source, pattern, **sizes):
+            rows = keep.tile([P, TILES * K], BF16, name=name)
             nc.sync.dma_start(out=rows[:].rearrange(pattern, **sizes), in_=source)
             return rows
 
         def load_x(c):
-            return load_rows(x_rows[c], "p f -> p f")
+            return load("x%d" % c, x_rows[c], "p f -> p f")
 
         def load_h(c):
-            h_sb = hrows_pool.tile([P, TILES * K], BF16, name="h_sb")
-            nc.sync.dma_start(out=h_sb[:], in_=h_rows[c])
-            return h_sb
+            return load("h%d" % c, h_rows[c], "p f -> p f")
 
-        def weight_codes(name):
-            codes = const.tile([P, PASSES * GROUP], U32, name=name + "_codes", align_bytes=64)
-            scales = const.tile([P, PASSES * GROUP], U8, name=name + "_scales", align_bytes=64)
+        def load_wu(g):
+            return load("wu%d" % g, wu_rows[g], "p (u f) -> p u f", u=2)
+
+        def load_wf(h):
+            return load("wf%d" % h, wf_rows[h], "p (b k) -> p b k", b=TILES)
+
+        h_sb = [load_h(0)]
+        wu_sb = [load_wu(0)]
+        x_sb = [load_x(0)]
+        wu_sb.append(load_wu(1))
+        h_sb.append(load_h(1))
+        x_sb.append(load_x(1))
+        wf_sb = [load_wf(0), load_wf(1)]
+        b_out_sb = keep.tile([P, OUT_DIM], BF16)
+        nc.sync.dma_start(out=b_out_sb[:], in_=b_out.partition_broadcast(P))
+        for c in range(2, CHUNKS):
+            h_sb.append(load_h(c))
+            x_sb.append(load_x(c))
+
+        def codes_and_scales(pool, name):
+            codes = pool.tile([P, PASSES * GROUP], U32, name=name + "_codes", align_bytes=64)
+            scales = pool.tile([P, PASSES * GROUP], U8, name=name + "_scales", align_bytes=64)
             return codes, scales
 
-        def quantise_x(x_sb):
-            codes = xcodes_pool.tile([P, PASSES * GROUP], U32, name="x_codes", align_bytes=64)
-            scales = xcodes_pool.tile([P, PASSES * GROUP], U8, name="x_scales", align_bytes=64)
-            quantise_group(nc, pools, x_sb[:], ident[:], codes[:], scales[:])
-            return codes, scales
+        def turn(rows, b, tag):
+            words = rows[:].bitcast(F32)
+            turned = psum.tile([P, PASSES, 2, P], F32, name="turned", tag=tag)
+            for g in range(PASSES):
+                for u in range(2):
+                    first = b * (K // 2) + (2 * g + u) * P
+                    nc.tensor.transpose(turned[:, g, u, :], words[:, first : first + P], ident[:])
+            return turned
 
-        def normalise(h_sb):
-            sum_sq = norm_pool.tile([P, TILES], F32, name="sum_sq")
-            for i in range(TILES):
-                squares = norm_pool.tile([P, K], BF16, name="squares")
-                nc.scalar.activation(
-                    out=squares[:],
-                    in_=h_sb[:, i * K : (i + 1) * K],
-                    func=ACT.Square,
-                    accum_out=sum_sq[:, i : i + 1],
-                )
-            mean_sq = norm_pool.tile([P, TILES], F32, name="mean_sq")
-            nc.gpsimd.tensor_scalar(
-                out=mean_sq[:], in0=sum_sq[:], scalar1=1.0 / K, scalar2=RMS_EPS, op0=ALU.mult, op1=ALU.add
+        def spread(copy, turned):
+            grouped = grouped_pool.tile([P, PASSES * P * PACK], BF16, name="grouped", align_bytes=64)
+            copy(
+                out=grouped[:].bitcast(F32).rearrange("p (g r u) -> p g r u", g=PASSES, u=2),
+                in_=turned[:].rearrange("p g u r -> p g r u"),
             )
-            rstd = norm_pool.tile([P, TILES], F32, name="rstd")
-            nc.gpsimd.tensor_tensor(out=rstd[:], in0=mean_sq[:], in1=minus_half[:], op=ALU.pow)
-            h_norm = norm_pool.tile([P, TILES, K], F32, name="h_norm")
-            for i in range(TILES):
-                nc.vector.tensor_scalar(
-                    out=h_norm[:, i, :].rearrange("p (q e m) -> p q e m", e=2, m=P),
-                    in0=h_sb[:, i * K : (i + 1) * K].rearrange("p (q m e) -> p q e m", m=P, e=2),
-                    scalar1=rstd[:, i : i + 1],
-                    scalar2=None,
-                    op0=ALU.mult,
-                )
-            return h_norm
+            return grouped
 
-        def gated_half(g2, x_q, h_norm, uv_codes, uv_scales):
-            x_codes, x_scales = x_q
-            w_codes, w_scales = wu_q[g2]
-            planes = gate_pool.tile([P, PACK, GROUP], BF16, name="planes")
-            for t in range(PACK):
-                j = PACK * g2 + t
-                z = psum.tile([P, GROUP], F32, name="z", tag="mx")
-                for g in range(PASSES):
-                    m_cols = slice(g * GROUP + t * P, g * GROUP + (t + 1) * P)
-                    n_cols = slice(g * GROUP, (g + 1) * GROUP)
-                    nc.tensor.matmul_mx(
-                        out=z[:],
-                        lhsT=w_codes[:, m_cols].bitcast(FP8X4),
-                        lhsT_scale=w_scales[:, m_cols],
-                        rhs=x_codes[:, n_cols].bitcast(FP8X4),
-                        rhs_scale=x_scales[:, n_cols],
-                        start=(g == 0),
-                        stop=(g == PASSES - 1),
-                    )
-                h_turned = psum.tile([P, GROUP], F32, name="h_turned", tag="turn")
+        def pack(grouped, operand, b):
+            codes, scales = operand
+            for g in range(PASSES):
+                cols = slice(g * GROUP + b * P, g * GROUP + (b + 1) * P)
+                nc.vector.quantize_mx(
+                    out=codes[:, cols].bitcast(FP8X4),
+                    scales=scales[:, cols],
+                    in_=grouped[:, g * P * PACK : (g + 1) * P * PACK],
+                )
+
+        def mx_product(acc, stationary, m_tile, moving):
+            for g in range(PASSES):
+                m_cols = slice(g * GROUP + m_tile * P, g * GROUP + (m_tile + 1) * P)
+                n_cols = slice(g * GROUP, (g + 1) * GROUP)
+                nc.tensor.matmul_mx(
+                    out=acc[:],
+                    lhsT=stationary[0][:, m_cols].bitcast(FP8X4),
+                    lhsT_scale=stationary[1][:, m_cols],
+                    rhs=moving[0][:, n_cols].bitcast(FP8X4),
+                    rhs_scale=moving[1][:, n_cols],
+                    start=(g == 0),
+                    stop=(g == PASSES - 1),
+                )
+
+        def mean_square(t):
+            c, i = divmod(t, TILES)
+            squares = norm_pool.tile([P, K], BF16, name="squares")
+            mean_sq = stats_pool.tile([P, 1], F32, name="mean_sq")
+            nc.scalar.activation(
+                out=squares[:],
+                in_=h_sb[c][:, i * K : (i + 1) * K],
+                func=ACT.Square,
+                scale=K**-0.5,
+                accum_out=mean_sq[:],
+            )
+            return mean_sq
+
+        def inverse_rms(mean_sq):
+            shifted = stats_pool.tile([P, 1], F32, name="shifted")
+            nc.gpsimd.tensor_scalar(
+                out=shifted[:], in0=mean_sq[:], scalar1=1.0, scalar2=RMS_EPS, op0=ALU.mult, op1=ALU.add
+            )
+            rstd = stats_pool.tile([P, 1], F32, name="rstd")
+            nc.gpsimd.tensor_tensor(out=rstd[:], in0=shifted[:], in1=minus_half[:], op=ALU.pow)
+            return rstd
+
+        def normalise(engine, t, rstd, h_norm):
+            c, i = divmod(t, TILES)
+            engine.tensor_scalar(
+                out=h_norm[:, i, :].rearrange("p (q e m) -> p q e m", e=2, m=P),
+                in0=h_sb[c][:, i * K : (i + 1) * K].rearrange("p (q m e) -> p q e m", m=P, e=2),
+                scalar1=rstd[:],
+                scalar2=0.0,
+                op0=ALU.mult,
+                op1=ALU.add,
+            )
+
+        wu_q = [codes_and_scales(keep, "wu0"), codes_and_scales(keep, "wu1")]
+        wf_q = [codes_and_scales(keep, "wf0"), codes_and_scales(keep, "wf1")]
+        x_q = {0: codes_and_scales(x_pool, "x")}
+        h_norm = {0: norm_pool.tile([P, TILES, K], F32, name="h_norm")}
+
+        first_rstd = [inverse_rms(mean_square(i)) for i in range(TILES)]
+        first_grouped = [spread(nc.vector.tensor_copy, turn(wu_sb[0], b, "acc")) for b in range(TILES)]
+        for b in range(TILES):
+            pack(first_grouped[b], wu_q[0], b)
+        for i in range(TILES):
+            grouped = spread(nc.scalar.copy, turn(x_sb[0], i, "turn"))
+            normalise(nc.vector, i, first_rstd[i], h_norm[0])
+            pack(grouped, x_q[0], i)
+
+        late_weights = [(wu_sb[1], wu_q[1], b) for b in range(TILES)]
+        for h in range(HALVES):
+            late_weights.extend([(wf_sb[h], wf_q[h], b) for b in range(TILES)])
+
+        uv_q = {}
+        planes = {}
+        for r in range(ROUNDS + LAG):
+            c, pair = divmod(r, PAIRS)
+            hidden = [2 * pair, 2 * pair + 1] if r < ROUNDS else []
+            g2 = pair // 2
+            ahead = r + AHEAD if r + AHEAD < TOKEN_TILES else None
+            behind = r - LAG if r >= LAG else None
+            weights = late_weights[2 * r : 2 * r + 2]
+
+            acc = []
+            if behind is not None:
+                for h in range(HALVES):
+                    acc.append(psum.tile([P, GROUP], F32, name="acc", tag="acc"))
+                    mx_product(acc[h], uv_q[behind // TILES], behind % TILES, wf_q[h])
+            z = []
+            for j in hidden:
+                z.append(psum.tile([P, GROUP], F32, name="z", tag="z"))
+                mx_product(z[-1], wu_q[g2], j % PACK, x_q[c])
+
+            h_turned = []
+            for j in hidden:
+                h_turned.append(psum.tile([P, GROUP], F32, name="h_turned", tag="ht"))
                 for i in range(TILES):
                     nc.tensor.transpose(
-                        h_turned[:, i * P : (i + 1) * P], h_norm[:, i, j * P : (j + 1) * P], ident[:]
+                        h_turned[-1][:, i * P : (i + 1) * P], h_norm[c][:, i, j * P : (j + 1) * P], ident[:]
                     )
-                u = silu_pool.tile([P, GROUP], F32, name="u")
-                nc.scalar.activation(out=u[:], in_=z[:], func=ACT.Silu, bias=bu_sb[:, j : j + 1], scale=1.0)
+            if ahead is not None:
+                x_turned = turn(x_sb[ahead // TILES], ahead % TILES, "turn")
+            w_turned = [turn(rows, b, "acc") for rows, operand, b in weights]
+
+            u = []
+            for n, j in enumerate(hidden):
+                u.append(silu_pool.tile([P, GROUP], F32, name="u"))
+                nc.scalar.activation(out=u[n][:], in_=z[n][:], func=ACT.Silu, bias=bu_sb[:, j : j + 1], scale=1.0)
+            if ahead is not None:
+                mean_sq = mean_square(ahead)
+                x_grouped = spread(nc.scalar.copy, x_turned)
+            w_grouped = [spread(nc.scalar.copy, w_turned[0])] if weights else []
+
+            if ahead is not None:
+                if ahead % TILES == 0:
+                    h_norm[ahead // TILES] = norm_pool.tile([P, TILES, K], F32, name="h_norm")
+                normalise(nc.gpsimd, ahead, inverse_rms(mean_sq), h_norm[ahead // TILES])
+
+            if behind is not None:
+                result = result_pool.tile([P, OUT_DIM], F32, name="result")
+                for h in range(HALVES):
+                    o_cols = slice(h * GROUP, (h + 1) * GROUP)
+                    nc.vector.tensor_tensor(out=result[:, o_cols], in0=acc[h][:], in1=b_out_sb[:, o_cols], op=ALU.add)
+                nc.sync.dma_start(out=out_rows[behind // TILES][:, behind % TILES, :], in_=result[:])
+            if hidden and pair % 2 == 0:
+                planes[g2] = gate_pool.tile([P, PACK, GROUP], BF16, name="planes")
+            for n, j in enumerate(hidden):
                 nc.vector.scalar_tensor_tensor(
-                    out=planes[:, t, :],
-                    in0=h_turned[:],
+                    out=planes[g2][:, j % PACK, :],
+                    in0=h_turned[n][:],
                     scalar=g_sb[:, j : j + 1],
-                    in1=u[:],
+                    in1=u[n][:],
                     op0=ALU.mult,
                     op1=ALU.mult,
                 )
-            uv_grouped = gate_pool.tile([P, GROUP, PACK], BF16, name="uv_grouped", align_bytes=64)
-            nc.vector.tensor_copy(out=uv_grouped[:], in_=planes[:].rearrange("p t r -> p r t"))
-            cols = slice(g2 * GROUP, (g2 + 1) * GROUP)
-            nc.vector.quantize_mx(
-                out=uv_codes[:, cols].bitcast(FP8X4),
-                scales=uv_scales[:, cols],
-                in_=uv_grouped[:].rearrange("p r t -> p (r t)"),
-            )
-
-        def project(c, uv_codes, uv_scales):
-            for i in range(TILES):
-                result = result_pool.tile([P, OUT_DIM], F32, name="result")
-                for h in range(OUT_DIM // GROUP):
-                    w_codes, w_scales = wf_q[h]
-                    acc = psum.tile([P, GROUP], F32, name="acc", tag="mx")
-                    for g in range(PASSES):
-                        m_cols = slice(g * GROUP + i * P, g * GROUP + (i + 1) * P)
-                        n_cols = slice(g * GROUP, (g + 1) * GROUP)
-                        nc.tensor.matmul_mx(
-                            out=acc[:],
-                            lhsT=uv_codes[:, m_cols].bitcast(FP8X4),
-                            lhsT_scale=uv_scales[:, m_cols],
-                            rhs=w_codes[:, n_cols].bitcast(FP8X4),
-                            rhs_scale=w_scales[:, n_cols],
-                            start=(g == 0),
-                            stop=(g == PASSES - 1),
-                        )
-                    o_cols = slice(h * GROUP, (h + 1) * GROUP)
-                    nc.vector.tensor_tensor(out=result[:, o_cols], in0=acc[:], in1=b_out_sb[:, o_cols], op=ALU.add)
-                nc.sync.dma_start(out=out_rows[c][:, i, :], in_=result[:])
-
-        wu_sb = [None, None]
-        wf_sb = [None, None]
-        wu_sb[0] = load_rows(wu_rows[0], "p (u f) -> p u f", u=2)
-        x_sb = load_x(0)
-        wu_sb[1] = load_rows(wu_rows[1], "p (u f) -> p u f", u=2)
-        h_sb = load_h(0)
-        bu_sb = const.tile([P, 2 * PACK], BF16)
-        nc.scalar.dma_start(
-            out=bu_sb[:].rearrange("p (q e) -> p q e", e=2), in_=bu.rearrange("(q p e) -> p q e", p=P, e=2)
-        )
-        g_sb = const.tile([P, 2 * PACK], BF16)
-        nc.scalar.dma_start(
-            out=g_sb[:].rearrange("p (q e) -> p q e", e=2), in_=g_norm.rearrange("(q p e) -> p q e", p=P, e=2)
-        )
-
-        wu_q = [weight_codes("wu0"), weight_codes("wu1")]
-        wf_q = [weight_codes("wf0"), weight_codes("wf1")]
-        quantise_group(nc, pools, wu_sb[0][:], ident[:], wu_q[0][0][:], wu_q[0][1][:])
-        x_q = quantise_x(x_sb)
-        quantise_group(nc, pools, wu_sb[1][:], ident[:], wu_q[1][0][:], wu_q[1][1][:])
-        h_norm = normalise(h_sb)
-
-        for h in range(2):
-            wf_sb[h] = load_rows(wf_rows[h], "p (b k) -> p b k", b=TILES)
-        b_out_sb = const.tile([P, OUT_DIM], BF16)
-        nc.sync.dma_start(out=b_out_sb[:], in_=b_out.partition_broadcast(P))
-
-        for c in range(CHUNKS):
-            if c + 1 < CHUNKS:
-                x_sb = load_x(c + 1)
-                h_sb = load_h(c + 1)
-            uv_codes = gate_pool.tile([P, PASSES * GROUP], U32, name="uv_codes", align_bytes=64)
-            uv_scales = gate_pool.tile([P, PASSES * GROUP], U8, name="uv_scales", align_bytes=64)
-            for g2 in range(PASSES):
-                gated_half(g2, x_q, h_norm, uv_codes, uv_scales)
-            if c == 0:
-                for h in range(2):
-                    quantise_group(nc, pools, wf_sb[h][:], ident[:], wf_q[h][0][:], wf_q[h][1][:])
-            if c + 1 < CHUNKS:
-                x_q = quantise_x(x_sb)
-                h_norm = normalise(h_sb)
-            project(c, uv_codes, uv_scales)
+            if weights:
+                w_grouped.append(spread(nc.vector.tensor_copy, w_turned[1]))
+            if ahead is not None:
+                if ahead % TILES == 0:
+                    x_q[ahead // TILES] = codes_and_scales(x_pool, "x")
+                pack(x_grouped, x_q[ahead // TILES], ahead % TILES)
+            for n, (rows, operand, b) in enumerate(weights):
+                pack(w_grouped[n], operand, b)
+            if hidden and pair % 2 == 1:
+                uv_grouped = gate_pool.tile([P, GROUP, PACK], BF16, name="uv_grouped", align_bytes=64)
+                nc.vector.tensor_copy(
+                    out=uv_grouped[:].rearrange("p (n i) t -> p n t i", i=4),
+                    in_=planes[g2][:].rearrange("p t (n i) -> p n t i", i=4),
+                )
+                if g2 == 0:
+                    uv_q[c] = codes_and_scales(gate_pool, "uv")
+                cols = slice(g2 * GROUP, (g2 + 1) * GROUP)
+                nc.vector.quantize_mx(
+                    out=uv_q[c][0][:, cols].bitcast(FP8X4),
+                    scales=uv_q[c][1][:, cols],
+                    in_=uv_grouped[:].rearrange("p r t -> p (r t)"),
+                )

@@ -170,16 +170,14 @@ def tile_hstu_pb_kernel(tc, x, h_attn, Wu, bu, g_norm, Wf, b_out, out):
             nc.gpsimd.tensor_tensor(out=rstd[:], in0=shifted[:], in1=minus_half[:], op=ALU.pow)
             return rstd
 
-        def normalise(engine, t, rstd, h_norm):
+        def normalise(t, rstd, h_norm):
             c, i = divmod(t, TILES)
-            engine.tensor_scalar(
-                out=h_norm[:, i, :].rearrange("p (q e m) -> p q e m", e=2, m=P),
-                in0=h_sb[c][:, i * K : (i + 1) * K].rearrange("p (q m e) -> p q e m", m=P, e=2),
-                scalar1=rstd[:],
-                scalar2=0.0,
-                op0=ALU.mult,
-                op1=ALU.add,
-            )
+            sorted_out = h_norm[:, i, :].rearrange("p (q e m) -> p q e m", e=2, m=P)
+            sorted_in = h_sb[c][:, i * K : (i + 1) * K].rearrange("p (q m e) -> p q e m", m=P, e=2)
+            if c == 0:
+                nc.vector.tensor_scalar(out=sorted_out, in0=sorted_in, scalar1=rstd[:], scalar2=None, op0=ALU.mult)
+            else:
+                nc.scalar.activation(out=sorted_out, in_=sorted_in, func=ACT.Copy, scale=rstd[:])
 
         wu_q = [codes_and_scales(keep, "wu0"), codes_and_scales(keep, "wu1")]
         wf_q = [codes_and_scales(keep, "wf0"), codes_and_scales(keep, "wf1")]
@@ -192,7 +190,7 @@ def tile_hstu_pb_kernel(tc, x, h_attn, Wu, bu, g_norm, Wf, b_out, out):
             pack(first_grouped[b], wu_q[0], b)
         for i in range(TILES):
             grouped = spread(nc.scalar.copy, turn(x_sb[0], i, "turn"))
-            normalise(nc.vector, i, first_rstd[i], h_norm[0])
+            normalise(i, first_rstd[i], h_norm[0])
             pack(grouped, x_q[0], i)
 
         late_weights = [(wu_sb[1], wu_q[1], b) for b in range(TILES)]
@@ -235,14 +233,11 @@ def tile_hstu_pb_kernel(tc, x, h_attn, Wu, bu, g_norm, Wf, b_out, out):
                 u.append(silu_pool.tile([P, GROUP], F32, name="u"))
                 nc.scalar.activation(out=u[n][:], in_=z[n][:], func=ACT.Silu, bias=bu_sb[:, j : j + 1], scale=1.0)
             if ahead is not None:
-                mean_sq = mean_square(ahead)
+                rstd = inverse_rms(mean_square(ahead))
                 x_grouped = spread(nc.scalar.copy, x_turned)
-            w_grouped = [spread(nc.scalar.copy, w_turned[0])] if weights else []
-
-            if ahead is not None:
                 if ahead % TILES == 0:
                     h_norm[ahead // TILES] = norm_pool.tile([P, TILES, K], F32, name="h_norm")
-                normalise(nc.gpsimd, ahead, inverse_rms(mean_sq), h_norm[ahead // TILES])
+                normalise(ahead, rstd, h_norm[ahead // TILES])
 
             if behind is not None:
                 result = result_pool.tile([P, OUT_DIM], F32, name="result")
@@ -261,8 +256,7 @@ def tile_hstu_pb_kernel(tc, x, h_attn, Wu, bu, g_norm, Wf, b_out, out):
                     op0=ALU.mult,
                     op1=ALU.mult,
                 )
-            if weights:
-                w_grouped.append(spread(nc.vector.tensor_copy, w_turned[1]))
+            w_grouped = [spread(nc.vector.tensor_copy, turned) for turned in w_turned]
             if ahead is not None:
                 if ahead % TILES == 0:
                     x_q[ahead // TILES] = codes_and_scales(x_pool, "x")

@@ -24,21 +24,31 @@ HALVES = OUT_DIM // GROUP
 TOKEN_TILES = TOKENS // P
 PAIRS = K // (2 * P)
 ROUNDS = CHUNKS * PAIRS
-AHEAD = 4
+WEIGHT_PAIRS = (K + OUT_DIM) // (2 * P)
+X_TURN = 6
+X_PACK = 5
+H_SQUARE = 6
+H_SCALE = 5
+W_AHEAD = 4
+WARM_UP = 6
 LAG = 6
 RMS_EPS = 1.1920928955078125e-07
 
 FLOPS = 2 * TOKENS * K * K + 2 * TOKENS * K * OUT_DIM
 
 
+def within(index, count):
+    return 0 <= index < count
+
+
 def tile_hstu_pb_kernel(tc, x, h_attn, Wu, bu, g_norm, Wf, b_out, out):
     nc = tc.nc
 
-    x_rows = x.flatten_outer_dims().rearrange("(c p i) k -> c p (i k)", p=P, i=TILES)
-    h_rows = h_attn.flatten_outer_dims().rearrange("(c p i) k -> c p (i k)", p=P, i=TILES)
-    out_rows = out.flatten_outer_dims().rearrange("(c p i) o -> c p i o", p=P, i=TILES)
-    wu_rows = Wu.rearrange("(g u p e) k -> g p u (e k)", g=PASSES, u=2, p=P, e=2)
-    wf_rows = Wf.rearrange("(h b p) k -> h p b k", h=HALVES, b=TILES, p=P)
+    x_rows = x.flatten_outer_dims().rearrange("(c p i) k -> c i p k", p=P, i=TILES)
+    h_rows = h_attn.flatten_outer_dims().rearrange("(c p i) k -> c i p k", p=P, i=TILES)
+    out_rows = out.flatten_outer_dims().rearrange("(c p i) o -> c i p o", p=P, i=TILES)
+    wu_rows = Wu.rearrange("(g u p e) k -> g u p (e k)", g=PASSES, u=2, p=P, e=2)
+    wf_rows = Wf.rearrange("(h v b p) k -> h v p b k", h=HALVES, v=2, b=2, p=P)
 
     with ExitStack() as stack:
 
@@ -46,21 +56,20 @@ def tile_hstu_pb_kernel(tc, x, h_attn, Wu, bu, g_norm, Wf, b_out, out):
             return stack.enter_context(tc.tile_pool(name=name, bufs=bufs))
 
         keep = open_pool("keep", 1)
-        grouped_pool = open_pool("grouped", 6)
+        grouped_pool = open_pool("grouped", 8)
         x_pool = open_pool("xcodes", 2)
         norm_pool = open_pool("norm", 2)
-        stats_pool = open_pool("stats", 4)
+        stats_pool = open_pool("stats", 6)
         silu_pool = open_pool("silu", 4)
         gate_pool = open_pool("gate", 2)
         result_pool = open_pool("result", 3)
-        psum = stack.enter_context(tc.psum_pool(name="psum", bufs=2))
+        psum = stack.enter_context(tc.psum_pool(name="psum", bufs=4))
         stack.enter_context(tc.manual_schedule())
 
         ident = keep.tile([P, P], F32)
         make_identity(nc, ident[:])
         minus_half = keep.tile([P, 1], F32)
         nc.gpsimd.memset(minus_half[:], -0.5)
-
         bu_sb = keep.tile([P, 2 * PACK], BF16)
         nc.scalar.dma_start(
             out=bu_sb[:].rearrange("p (q e) -> p q e", e=2), in_=bu.rearrange("(q p e) -> p q e", p=P, e=2)
@@ -72,44 +81,39 @@ def tile_hstu_pb_kernel(tc, x, h_attn, Wu, bu, g_norm, Wf, b_out, out):
         table_warm = keep.tile([P, 1], F32)
         nc.scalar.activation(out=table_warm[:], in_=minus_half[:], func=ACT.Silu)
 
-        def load(name, source, pattern, **sizes):
-            rows = keep.tile([P, TILES * K], BF16, name=name)
-            nc.sync.dma_start(out=rows[:].rearrange(pattern, **sizes), in_=source)
-            return rows
-
-        def load_x(c):
-            return load("x%d" % c, x_rows[c], "p f -> p f")
-
-        def load_h(c):
-            return load("h%d" % c, h_rows[c], "p f -> p f")
-
-        def load_wu(g):
-            return load("wu%d" % g, wu_rows[g], "p (u f) -> p u f", u=2)
-
-        def load_wf(h):
-            return load("wf%d" % h, wf_rows[h], "p (b k) -> p b k", b=TILES)
-
-        h_sb = [load_h(0)]
-        wu_sb = [load_wu(0)]
-        x_sb = [load_x(0)]
-        wu_sb.append(load_wu(1))
-        h_sb.append(load_h(1))
-        x_sb.append(load_x(1))
-        wf_sb = [load_wf(0), load_wf(1)]
+        x_sb = [keep.tile([P, TILES * K], BF16, name="x%d" % c) for c in range(CHUNKS)]
+        h_sb = [keep.tile([P, TILES * K], BF16, name="h%d" % c) for c in range(CHUNKS)]
+        w_sb = [keep.tile([P, TILES * K], BF16, name="w%d" % n) for n in range(PASSES + HALVES)]
         b_out_sb = keep.tile([P, OUT_DIM], BF16)
-        nc.sync.dma_start(out=b_out_sb[:], in_=b_out.partition_broadcast(P))
-        for c in range(2, CHUNKS):
-            h_sb.append(load_h(c))
-            x_sb.append(load_x(c))
+
+        def tile_of(rows, i):
+            return rows[:, i * K : (i + 1) * K]
+
+        for r in range(-WARM_UP, ROUNDS):
+            if within(r + H_SQUARE, TOKEN_TILES):
+                c, i = divmod(r + H_SQUARE, TILES)
+                nc.sync.dma_start(out=tile_of(h_sb[c], i), in_=h_rows[c][i])
+            if within(r + X_TURN, TOKEN_TILES):
+                c, i = divmod(r + X_TURN, TILES)
+                nc.sync.dma_start(out=tile_of(x_sb[c], i), in_=x_rows[c][i])
+            if within(r + W_AHEAD, WEIGHT_PAIRS):
+                n, v = divmod(r + W_AHEAD, 2)
+                both = w_sb[n][:, 2 * v * K : (2 * v + 2) * K]
+                if n < PASSES:
+                    nc.sync.dma_start(out=both, in_=wu_rows[n][v])
+                else:
+                    nc.sync.dma_start(out=both.rearrange("p (b k) -> p b k", b=2), in_=wf_rows[n - PASSES][v])
+            if r + W_AHEAD == WEIGHT_PAIRS:
+                nc.sync.dma_start(out=b_out_sb[:], in_=b_out.partition_broadcast(P))
 
         def codes_and_scales(pool, name):
             codes = pool.tile([P, PASSES * GROUP], U32, name=name + "_codes", align_bytes=64)
             scales = pool.tile([P, PASSES * GROUP], U8, name=name + "_scales", align_bytes=64)
             return codes, scales
 
-        def turn(rows, b, tag):
+        def turn(rows, b, ring):
             words = rows[:].bitcast(F32)
-            turned = psum.tile([P, PASSES, 2, P], F32, name="turned", tag=tag)
+            turned = psum.tile([P, PASSES, 2, P], F32, name="turned", tag=ring)
             for g in range(PASSES):
                 for u in range(2):
                     first = b * (K // 2) + (2 * g + u) * P
@@ -134,7 +138,8 @@ def tile_hstu_pb_kernel(tc, x, h_attn, Wu, bu, g_norm, Wf, b_out, out):
                     in_=grouped[:, g * P * PACK : (g + 1) * P * PACK],
                 )
 
-        def mx_product(acc, stationary, m_tile, moving):
+        def mx_product(stationary, m_tile, moving):
+            acc = psum.tile([P, GROUP], F32, name="acc", tag="mx")
             for g in range(PASSES):
                 m_cols = slice(g * GROUP + m_tile * P, g * GROUP + (m_tile + 1) * P)
                 n_cols = slice(g * GROUP, (g + 1) * GROUP)
@@ -147,21 +152,18 @@ def tile_hstu_pb_kernel(tc, x, h_attn, Wu, bu, g_norm, Wf, b_out, out):
                     start=(g == 0),
                     stop=(g == PASSES - 1),
                 )
+            return acc
 
-        def mean_square(t):
-            c, i = divmod(t, TILES)
+        def inverse_rms(t):
             squares = norm_pool.tile([P, K], BF16, name="squares")
             mean_sq = stats_pool.tile([P, 1], F32, name="mean_sq")
             nc.scalar.activation(
                 out=squares[:],
-                in_=h_sb[c][:, i * K : (i + 1) * K],
+                in_=tile_of(h_sb[t // TILES], t % TILES),
                 func=ACT.Square,
                 scale=K**-0.5,
                 accum_out=mean_sq[:],
             )
-            return mean_sq
-
-        def inverse_rms(mean_sq):
             shifted = stats_pool.tile([P, 1], F32, name="shifted")
             nc.gpsimd.tensor_scalar(
                 out=shifted[:], in0=mean_sq[:], scalar1=1.0, scalar2=RMS_EPS, op0=ALU.mult, op1=ALU.add
@@ -170,81 +172,77 @@ def tile_hstu_pb_kernel(tc, x, h_attn, Wu, bu, g_norm, Wf, b_out, out):
             nc.gpsimd.tensor_tensor(out=rstd[:], in0=shifted[:], in1=minus_half[:], op=ALU.pow)
             return rstd
 
-        def normalise(t, rstd, h_norm):
-            c, i = divmod(t, TILES)
-            sorted_out = h_norm[:, i, :].rearrange("p (q e m) -> p q e m", e=2, m=P)
-            sorted_in = h_sb[c][:, i * K : (i + 1) * K].rearrange("p (q m e) -> p q e m", m=P, e=2)
-            if c == 0:
-                nc.vector.tensor_scalar(out=sorted_out, in0=sorted_in, scalar1=rstd[:], scalar2=None, op0=ALU.mult)
-            else:
-                nc.scalar.activation(out=sorted_out, in_=sorted_in, func=ACT.Copy, scale=rstd[:])
+        def normalise(engine, t, rstd, h_norm):
+            engine.tensor_scalar(
+                out=h_norm[:, t % TILES, :].rearrange("p (q e m) -> p q e m", e=2, m=P),
+                in0=tile_of(h_sb[t // TILES], t % TILES).rearrange("p (q m e) -> p q e m", m=P, e=2),
+                scalar1=rstd[:],
+                scalar2=0.0,
+                op0=ALU.mult,
+                op1=ALU.add,
+            )
 
-        wu_q = [codes_and_scales(keep, "wu0"), codes_and_scales(keep, "wu1")]
-        wf_q = [codes_and_scales(keep, "wf0"), codes_and_scales(keep, "wf1")]
-        x_q = {0: codes_and_scales(x_pool, "x")}
-        h_norm = {0: norm_pool.tile([P, TILES, K], F32, name="h_norm")}
-
-        first_rstd = [inverse_rms(mean_square(i)) for i in range(TILES)]
-        first_grouped = [spread(nc.vector.tensor_copy, turn(wu_sb[0], b, "acc")) for b in range(TILES)]
-        for b in range(TILES):
-            pack(first_grouped[b], wu_q[0], b)
-        for i in range(TILES):
-            grouped = spread(nc.scalar.copy, turn(x_sb[0], i, "turn"))
-            normalise(i, first_rstd[i], h_norm[0])
-            pack(grouped, x_q[0], i)
-
-        late_weights = [(wu_sb[1], wu_q[1], b) for b in range(TILES)]
-        for h in range(HALVES):
-            late_weights.extend([(wf_sb[h], wf_q[h], b) for b in range(TILES)])
-
+        w_q = [codes_and_scales(keep, "w%d" % n) for n in range(PASSES + HALVES)]
+        x_q = {}
+        h_norm = {}
         uv_q = {}
         planes = {}
-        for r in range(ROUNDS + LAG):
-            c, pair = divmod(r, PAIRS)
-            hidden = [2 * pair, 2 * pair + 1] if r < ROUNDS else []
-            g2 = pair // 2
-            ahead = r + AHEAD if r + AHEAD < TOKEN_TILES else None
-            behind = r - LAG if r >= LAG else None
-            weights = late_weights[2 * r : 2 * r + 2]
+        x_grouped = {}
+        rstd = {}
 
+        for r in range(-WARM_UP, ROUNDS + LAG):
+            chunk, pair = divmod(r, PAIRS)
+            hidden = [2 * pair, 2 * pair + 1] if within(r, ROUNDS) else []
+            g2 = pair // 2
+            behind = r - LAG
+            x_new = r + X_TURN
+            x_ready = r + X_PACK
+            h_new = r + H_SQUARE
+            h_ready = r + H_SCALE
+            w_new = r + W_AHEAD
+            early = x_new < TILES
+
+            z = [mx_product(w_q[g2], j % PACK, x_q[chunk]) for j in hidden]
             acc = []
-            if behind is not None:
-                for h in range(HALVES):
-                    acc.append(psum.tile([P, GROUP], F32, name="acc", tag="acc"))
-                    mx_product(acc[h], uv_q[behind // TILES], behind % TILES, wf_q[h])
-            z = []
-            for j in hidden:
-                z.append(psum.tile([P, GROUP], F32, name="z", tag="z"))
-                mx_product(z[-1], wu_q[g2], j % PACK, x_q[c])
+            if within(behind, TOKEN_TILES):
+                acc = [mx_product(uv_q[behind // TILES], behind % TILES, w_q[PASSES + h]) for h in range(HALVES)]
 
             h_turned = []
             for j in hidden:
-                h_turned.append(psum.tile([P, GROUP], F32, name="h_turned", tag="ht"))
+                h_turned.append(psum.tile([P, GROUP], F32, name="h_turned", tag="turn"))
                 for i in range(TILES):
                     nc.tensor.transpose(
-                        h_turned[-1][:, i * P : (i + 1) * P], h_norm[c][:, i, j * P : (j + 1) * P], ident[:]
+                        h_turned[-1][:, i * P : (i + 1) * P], h_norm[chunk][:, i, j * P : (j + 1) * P], ident[:]
                     )
-            if ahead is not None:
-                x_turned = turn(x_sb[ahead // TILES], ahead % TILES, "turn")
-            w_turned = [turn(rows, b, "acc") for rows, operand, b in weights]
+            if within(x_new, TOKEN_TILES):
+                x_turned = turn(x_sb[x_new // TILES], x_new % TILES, "turn")
+            w_turned = []
+            if within(w_new, WEIGHT_PAIRS):
+                w_tiles = [2 * (w_new % 2), 2 * (w_new % 2) + 1]
+                w_turned = [turn(w_sb[w_new // 2], b, "mx") for b in w_tiles]
 
             u = []
             for n, j in enumerate(hidden):
                 u.append(silu_pool.tile([P, GROUP], F32, name="u"))
                 nc.scalar.activation(out=u[n][:], in_=z[n][:], func=ACT.Silu, bias=bu_sb[:, j : j + 1], scale=1.0)
-            if ahead is not None:
-                rstd = inverse_rms(mean_square(ahead))
-                x_grouped = spread(nc.scalar.copy, x_turned)
-                if ahead % TILES == 0:
-                    h_norm[ahead // TILES] = norm_pool.tile([P, TILES, K], F32, name="h_norm")
-                normalise(ahead, rstd, h_norm[ahead // TILES])
+            if within(h_new, TOKEN_TILES):
+                rstd[h_new] = inverse_rms(h_new)
+            if within(x_new, TOKEN_TILES) and not early:
+                x_grouped[x_new] = spread(nc.scalar.copy, x_turned)
+            w_grouped = [spread(nc.scalar.copy, w_turned[0])] if w_turned else []
 
-            if behind is not None:
+            if within(h_ready, TOKEN_TILES):
+                if h_ready % TILES == 0:
+                    h_norm[h_ready // TILES] = norm_pool.tile([P, TILES, K], F32, name="h_norm")
+                if h_ready >= TILES:
+                    normalise(nc.gpsimd, h_ready, rstd[h_ready], h_norm[h_ready // TILES])
+
+            if acc:
                 result = result_pool.tile([P, OUT_DIM], F32, name="result")
                 for h in range(HALVES):
                     o_cols = slice(h * GROUP, (h + 1) * GROUP)
                     nc.vector.tensor_tensor(out=result[:, o_cols], in0=acc[h][:], in1=b_out_sb[:, o_cols], op=ALU.add)
-                nc.sync.dma_start(out=out_rows[behind // TILES][:, behind % TILES, :], in_=result[:])
+                nc.sync.dma_start(out=out_rows[behind // TILES][behind % TILES], in_=result[:])
             if hidden and pair % 2 == 0:
                 planes[g2] = gate_pool.tile([P, PACK, GROUP], BF16, name="planes")
             for n, j in enumerate(hidden):
@@ -256,13 +254,18 @@ def tile_hstu_pb_kernel(tc, x, h_attn, Wu, bu, g_norm, Wf, b_out, out):
                     op0=ALU.mult,
                     op1=ALU.mult,
                 )
-            w_grouped = [spread(nc.vector.tensor_copy, turned) for turned in w_turned]
-            if ahead is not None:
-                if ahead % TILES == 0:
-                    x_q[ahead // TILES] = codes_and_scales(x_pool, "x")
-                pack(x_grouped, x_q[ahead // TILES], ahead % TILES)
-            for n, (rows, operand, b) in enumerate(weights):
-                pack(w_grouped[n], operand, b)
+            if within(x_new, TOKEN_TILES) and early:
+                x_grouped[x_new] = spread(nc.vector.tensor_copy, x_turned)
+            if w_turned:
+                w_grouped.append(spread(nc.vector.tensor_copy, w_turned[1]))
+            if within(h_ready, TILES):
+                normalise(nc.vector, h_ready, rstd[h_ready], h_norm[0])
+            if within(x_ready, TOKEN_TILES):
+                if x_ready % TILES == 0:
+                    x_q[x_ready // TILES] = codes_and_scales(x_pool, "x")
+                pack(x_grouped[x_ready], x_q[x_ready // TILES], x_ready % TILES)
+            for n in range(len(w_turned)):
+                pack(w_grouped[n], w_q[w_new // 2], w_tiles[n])
             if hidden and pair % 2 == 1:
                 uv_grouped = gate_pool.tile([P, GROUP, PACK], BF16, name="uv_grouped", align_bytes=64)
                 nc.vector.tensor_copy(
@@ -270,10 +273,10 @@ def tile_hstu_pb_kernel(tc, x, h_attn, Wu, bu, g_norm, Wf, b_out, out):
                     in_=planes[g2][:].rearrange("p t (n i) -> p n t i", i=4),
                 )
                 if g2 == 0:
-                    uv_q[c] = codes_and_scales(gate_pool, "uv")
+                    uv_q[chunk] = codes_and_scales(gate_pool, "uv")
                 cols = slice(g2 * GROUP, (g2 + 1) * GROUP)
                 nc.vector.quantize_mx(
-                    out=uv_q[c][0][:, cols].bitcast(FP8X4),
-                    scales=uv_q[c][1][:, cols],
+                    out=uv_q[chunk][0][:, cols].bitcast(FP8X4),
+                    scales=uv_q[chunk][1][:, cols],
                     in_=uv_grouped[:].rearrange("p r t -> p (r t)"),
                 )

@@ -173,14 +173,17 @@ def tile_hstu_pb_kernel(tc, x, h_attn, Wu, bu, g_norm, Wf, b_out, out):
             return rstd
 
         def normalise(engine, t, rstd, h_norm):
-            engine.tensor_scalar(
-                out=h_norm[:, t % TILES, :].rearrange("p (q e m) -> p q e m", e=2, m=P),
-                in0=tile_of(h_sb[t // TILES], t % TILES).rearrange("p (q m e) -> p q e m", m=P, e=2),
-                scalar1=rstd[:],
-                scalar2=0.0,
-                op0=ALU.mult,
-                op1=ALU.add,
-            )
+            sorted_out = h_norm[:, t % TILES, :].rearrange("p (q e m) -> p q e m", e=2, m=P)
+            sorted_in = tile_of(h_sb[t // TILES], t % TILES).rearrange("p (q m e) -> p q e m", m=P, e=2)
+            for q in range(0, PACK, 2):
+                engine.tensor_scalar(
+                    out=sorted_out[:, q : q + 2],
+                    in0=sorted_in[:, q : q + 2],
+                    scalar1=rstd[:],
+                    scalar2=0.0,
+                    op0=ALU.mult,
+                    op1=ALU.add,
+                )
 
         w_q = [codes_and_scales(keep, "w%d" % n) for n in range(PASSES + HALVES)]
         x_q = {}
@@ -242,7 +245,7 @@ def tile_hstu_pb_kernel(tc, x, h_attn, Wu, bu, g_norm, Wf, b_out, out):
                 for h in range(HALVES):
                     o_cols = slice(h * GROUP, (h + 1) * GROUP)
                     nc.vector.tensor_tensor(out=result[:, o_cols], in0=acc[h][:], in1=b_out_sb[:, o_cols], op=ALU.add)
-                nc.sync.dma_start(out=out_rows[behind // TILES][behind % TILES], in_=result[:])
+                    nc.sync.dma_start(out=out_rows[behind // TILES][behind % TILES][:, o_cols], in_=result[:, o_cols])
             if hidden and pair % 2 == 0:
                 planes[g2] = gate_pool.tile([P, PACK, GROUP], BF16, name="planes")
             for n, j in enumerate(hidden):
@@ -266,17 +269,20 @@ def tile_hstu_pb_kernel(tc, x, h_attn, Wu, bu, g_norm, Wf, b_out, out):
                 pack(x_grouped[x_ready], x_q[x_ready // TILES], x_ready % TILES)
             for n in range(len(w_turned)):
                 pack(w_grouped[n], w_q[w_new // 2], w_tiles[n])
+            if within(r - 1, ROUNDS) and pair % 2 == 0:
+                done_chunk, done_pair = divmod(r - 1, PAIRS)
+                done_pass = done_pair // 2
+                if done_pass == 0:
+                    uv_q[done_chunk] = codes_and_scales(gate_pool, "uv")
+                cols = slice(done_pass * GROUP, (done_pass + 1) * GROUP)
+                nc.vector.quantize_mx(
+                    out=uv_q[done_chunk][0][:, cols].bitcast(FP8X4),
+                    scales=uv_q[done_chunk][1][:, cols],
+                    in_=uv_grouped[:].rearrange("p r t -> p (r t)"),
+                )
             if hidden and pair % 2 == 1:
                 uv_grouped = gate_pool.tile([P, GROUP, PACK], BF16, name="uv_grouped", align_bytes=64)
                 nc.vector.tensor_copy(
                     out=uv_grouped[:].rearrange("p (n i) t -> p n t i", i=4),
                     in_=planes[g2][:].rearrange("p t (n i) -> p n t i", i=4),
-                )
-                if g2 == 0:
-                    uv_q[chunk] = codes_and_scales(gate_pool, "uv")
-                cols = slice(g2 * GROUP, (g2 + 1) * GROUP)
-                nc.vector.quantize_mx(
-                    out=uv_q[chunk][0][:, cols].bitcast(FP8X4),
-                    scales=uv_q[chunk][1][:, cols],
-                    in_=uv_grouped[:].rearrange("p r t -> p (r t)"),
                 )

@@ -22,9 +22,11 @@ TILES = GROUP // P
 CHUNKS = TOKENS // GROUP
 HALVES = OUT_DIM // GROUP
 TOKEN_TILES = TOKENS // P
-PAIRS = K // (2 * P)
+HIDDEN_TILES = K // P
+PAIRS = HIDDEN_TILES // 2
 ROUNDS = CHUNKS * PAIRS
-WEIGHT_PAIRS = (K + OUT_DIM) // (2 * P)
+WEIGHT_BLOCKS = PASSES + HALVES
+WEIGHT_PAIRS = 2 * WEIGHT_BLOCKS
 X_TURN = 6
 X_PACK = 5
 H_SQUARE = 6
@@ -32,6 +34,7 @@ H_SCALE = 5
 W_AHEAD = 4
 WARM_UP = 6
 LAG = 6
+TOKEN_RUN = 4
 RMS_EPS = 1.1920928955078125e-07
 
 FLOPS = 2 * TOKENS * K * K + 2 * TOKENS * K * OUT_DIM
@@ -70,11 +73,11 @@ def tile_hstu_pb_kernel(tc, x, h_attn, Wu, bu, g_norm, Wf, b_out, out):
         make_identity(nc, ident[:])
         minus_half = keep.tile([P, 1], F32)
         nc.gpsimd.memset(minus_half[:], -0.5)
-        bu_sb = keep.tile([P, 2 * PACK], BF16)
+        bu_sb = keep.tile([P, HIDDEN_TILES], BF16)
         nc.scalar.dma_start(
             out=bu_sb[:].rearrange("p (q e) -> p q e", e=2), in_=bu.rearrange("(q p e) -> p q e", p=P, e=2)
         )
-        g_sb = keep.tile([P, 2 * PACK], BF16)
+        g_sb = keep.tile([P, HIDDEN_TILES], BF16)
         nc.scalar.dma_start(
             out=g_sb[:].rearrange("p (q e) -> p q e", e=2), in_=g_norm.rearrange("(q p e) -> p q e", p=P, e=2)
         )
@@ -83,7 +86,7 @@ def tile_hstu_pb_kernel(tc, x, h_attn, Wu, bu, g_norm, Wf, b_out, out):
 
         x_sb = [keep.tile([P, TILES * K], BF16, name="x%d" % c) for c in range(CHUNKS)]
         h_sb = [keep.tile([P, TILES * K], BF16, name="h%d" % c) for c in range(CHUNKS)]
-        w_sb = [keep.tile([P, TILES * K], BF16, name="w%d" % n) for n in range(PASSES + HALVES)]
+        w_sb = [keep.tile([P, TILES * K], BF16, name="w%d" % block) for block in range(WEIGHT_BLOCKS)]
         b_out_sb = keep.tile([P, OUT_DIM], BF16)
 
         def tile_of(rows, i):
@@ -97,12 +100,12 @@ def tile_hstu_pb_kernel(tc, x, h_attn, Wu, bu, g_norm, Wf, b_out, out):
                 c, i = divmod(r + X_TURN, TILES)
                 nc.sync.dma_start(out=tile_of(x_sb[c], i), in_=x_rows[c][i])
             if within(r + W_AHEAD, WEIGHT_PAIRS):
-                n, v = divmod(r + W_AHEAD, 2)
-                both = w_sb[n][:, 2 * v * K : (2 * v + 2) * K]
-                if n < PASSES:
-                    nc.sync.dma_start(out=both, in_=wu_rows[n][v])
+                block, v = divmod(r + W_AHEAD, 2)
+                both = w_sb[block][:, 2 * v * K : (2 * v + 2) * K]
+                if block < PASSES:
+                    nc.sync.dma_start(out=both, in_=wu_rows[block][v])
                 else:
-                    nc.sync.dma_start(out=both.rearrange("p (b k) -> p b k", b=2), in_=wf_rows[n - PASSES][v])
+                    nc.sync.dma_start(out=both.rearrange("p (b k) -> p b k", b=2), in_=wf_rows[block - PASSES][v])
             if r + W_AHEAD == WEIGHT_PAIRS:
                 nc.sync.dma_start(out=b_out_sb[:], in_=b_out.partition_broadcast(P))
 
@@ -139,12 +142,12 @@ def tile_hstu_pb_kernel(tc, x, h_attn, Wu, bu, g_norm, Wf, b_out, out):
                 )
 
         def mx_product(stationary, m_tile, moving):
-            acc = psum.tile([P, GROUP], F32, name="acc", tag="mx")
+            bank = psum.tile([P, GROUP], F32, name="acc", tag="mx")
             for g in range(PASSES):
                 m_cols = slice(g * GROUP + m_tile * P, g * GROUP + (m_tile + 1) * P)
                 n_cols = slice(g * GROUP, (g + 1) * GROUP)
                 nc.tensor.matmul_mx(
-                    out=acc[:],
+                    out=bank[:],
                     lhsT=stationary[0][:, m_cols].bitcast(FP8X4),
                     lhsT_scale=stationary[1][:, m_cols],
                     rhs=moving[0][:, n_cols].bitcast(FP8X4),
@@ -152,7 +155,7 @@ def tile_hstu_pb_kernel(tc, x, h_attn, Wu, bu, g_norm, Wf, b_out, out):
                     start=(g == 0),
                     stop=(g == PASSES - 1),
                 )
-            return acc
+            return bank
 
         def inverse_rms(t):
             squares = norm_pool.tile([P, K], BF16, name="squares")
@@ -172,26 +175,29 @@ def tile_hstu_pb_kernel(tc, x, h_attn, Wu, bu, g_norm, Wf, b_out, out):
             nc.gpsimd.tensor_tensor(out=rstd[:], in0=shifted[:], in1=minus_half[:], op=ALU.pow)
             return rstd
 
-        def normalise(engine, t, rstd, h_norm):
-            sorted_out = h_norm[:, t % TILES, :].rearrange("p (q e m) -> p q e m", e=2, m=P)
+        def sorted_half(t, half):
+            q_range = slice(half * PAIRS // 2, (half + 1) * PAIRS // 2)
+            sorted_out = h_norm_of[t // TILES][:, t % TILES, :].rearrange("p (q e m) -> p q e m", e=2, m=P)
             sorted_in = tile_of(h_sb[t // TILES], t % TILES).rearrange("p (q m e) -> p q e m", m=P, e=2)
-            for q in range(0, PACK, 2):
-                engine.tensor_scalar(
-                    out=sorted_out[:, q : q + 2],
-                    in0=sorted_in[:, q : q + 2],
-                    scalar1=rstd[:],
-                    scalar2=0.0,
-                    op0=ALU.mult,
-                    op1=ALU.add,
-                )
+            return sorted_out[:, q_range], sorted_in[:, q_range]
 
-        w_q = [codes_and_scales(keep, "w%d" % n) for n in range(PASSES + HALVES)]
+        def normalise(engine, t, half):
+            sorted_out, sorted_in = sorted_half(t, half)
+            engine.tensor_scalar(
+                out=sorted_out, in0=sorted_in, scalar1=rstd_of[t][:], scalar2=0.0, op0=ALU.mult, op1=ALU.add
+            )
+
+        def normalise_on_scalar(t, half):
+            sorted_out, sorted_in = sorted_half(t, half)
+            nc.scalar.activation(out=sorted_out, in_=sorted_in, func=ACT.Copy, scale=rstd_of[t][:])
+
+        w_q = [codes_and_scales(keep, "w%d" % block) for block in range(WEIGHT_BLOCKS)]
         x_q = {}
-        h_norm = {}
         uv_q = {}
+        h_norm_of = {}
         planes = {}
         x_grouped = {}
-        rstd = {}
+        rstd_of = {}
 
         for r in range(-WARM_UP, ROUNDS + LAG):
             chunk, pair = divmod(r, PAIRS)
@@ -206,16 +212,18 @@ def tile_hstu_pb_kernel(tc, x, h_attn, Wu, bu, g_norm, Wf, b_out, out):
             early = x_new < TILES
 
             z = [mx_product(w_q[g2], j % PACK, x_q[chunk]) for j in hidden]
-            acc = []
+            projected = []
             if within(behind, TOKEN_TILES):
-                acc = [mx_product(uv_q[behind // TILES], behind % TILES, w_q[PASSES + h]) for h in range(HALVES)]
+                projected = [
+                    mx_product(uv_q[behind // TILES], behind % TILES, w_q[PASSES + h]) for h in range(HALVES)
+                ]
 
             h_turned = []
             for j in hidden:
                 h_turned.append(psum.tile([P, GROUP], F32, name="h_turned", tag="turn"))
                 for i in range(TILES):
                     nc.tensor.transpose(
-                        h_turned[-1][:, i * P : (i + 1) * P], h_norm[chunk][:, i, j * P : (j + 1) * P], ident[:]
+                        h_turned[-1][:, i * P : (i + 1) * P], h_norm_of[chunk][:, i, j * P : (j + 1) * P], ident[:]
                     )
             if within(x_new, TOKEN_TILES):
                 x_turned = turn(x_sb[x_new // TILES], x_new % TILES, "turn")
@@ -225,50 +233,54 @@ def tile_hstu_pb_kernel(tc, x, h_attn, Wu, bu, g_norm, Wf, b_out, out):
                 w_turned = [turn(w_sb[w_new // 2], b, "mx") for b in w_tiles]
 
             u = []
-            for n, j in enumerate(hidden):
+            for s, j in enumerate(hidden):
                 u.append(silu_pool.tile([P, GROUP], F32, name="u"))
-                nc.scalar.activation(out=u[n][:], in_=z[n][:], func=ACT.Silu, bias=bu_sb[:, j : j + 1], scale=1.0)
+                nc.scalar.activation(out=u[s][:], in_=z[s][:], func=ACT.Silu, bias=bu_sb[:, j : j + 1], scale=1.0)
             if within(h_new, TOKEN_TILES):
-                rstd[h_new] = inverse_rms(h_new)
+                rstd_of[h_new] = inverse_rms(h_new)
             if within(x_new, TOKEN_TILES) and not early:
                 x_grouped[x_new] = spread(nc.scalar.copy, x_turned)
-            w_grouped = [spread(nc.scalar.copy, w_turned[0])] if w_turned else []
+            w_grouped = [spread(nc.scalar.copy, w_turned[0])] if w_turned and r < 0 else []
 
             if within(h_ready, TOKEN_TILES):
                 if h_ready % TILES == 0:
-                    h_norm[h_ready // TILES] = norm_pool.tile([P, TILES, K], F32, name="h_norm")
+                    h_norm_of[h_ready // TILES] = norm_pool.tile([P, TILES, K], F32, name="h_norm")
                 if h_ready >= TILES:
-                    normalise(nc.gpsimd, h_ready, rstd[h_ready], h_norm[h_ready // TILES])
+                    normalise(nc.gpsimd, h_ready, 0)
+                    normalise_on_scalar(h_ready, 1)
 
-            if acc:
+            if projected:
                 result = result_pool.tile([P, OUT_DIM], F32, name="result")
                 for h in range(HALVES):
                     o_cols = slice(h * GROUP, (h + 1) * GROUP)
-                    nc.vector.tensor_tensor(out=result[:, o_cols], in0=acc[h][:], in1=b_out_sb[:, o_cols], op=ALU.add)
+                    nc.vector.tensor_tensor(
+                        out=result[:, o_cols], in0=projected[h][:], in1=b_out_sb[:, o_cols], op=ALU.add
+                    )
                     nc.sync.dma_start(out=out_rows[behind // TILES][behind % TILES][:, o_cols], in_=result[:, o_cols])
             if hidden and pair % 2 == 0:
                 planes[g2] = gate_pool.tile([P, PACK, GROUP], BF16, name="planes")
-            for n, j in enumerate(hidden):
+            for s, j in enumerate(hidden):
                 nc.vector.scalar_tensor_tensor(
                     out=planes[g2][:, j % PACK, :],
-                    in0=h_turned[n][:],
+                    in0=h_turned[s][:],
                     scalar=g_sb[:, j : j + 1],
-                    in1=u[n][:],
+                    in1=u[s][:],
                     op0=ALU.mult,
                     op1=ALU.mult,
                 )
             if within(x_new, TOKEN_TILES) and early:
                 x_grouped[x_new] = spread(nc.vector.tensor_copy, x_turned)
-            if w_turned:
-                w_grouped.append(spread(nc.vector.tensor_copy, w_turned[1]))
+            for turned in w_turned[len(w_grouped) :]:
+                w_grouped.append(spread(nc.vector.tensor_copy, turned))
             if within(h_ready, TILES):
-                normalise(nc.vector, h_ready, rstd[h_ready], h_norm[0])
+                normalise(nc.vector, h_ready, 0)
+                normalise(nc.vector, h_ready, 1)
             if within(x_ready, TOKEN_TILES):
                 if x_ready % TILES == 0:
                     x_q[x_ready // TILES] = codes_and_scales(x_pool, "x")
                 pack(x_grouped[x_ready], x_q[x_ready // TILES], x_ready % TILES)
-            for n in range(len(w_turned)):
-                pack(w_grouped[n], w_q[w_new // 2], w_tiles[n])
+            for s in range(len(w_turned)):
+                pack(w_grouped[s], w_q[w_new // 2], w_tiles[s])
             if within(r - 1, ROUNDS) and pair % 2 == 0:
                 done_chunk, done_pair = divmod(r - 1, PAIRS)
                 done_pass = done_pair // 2
@@ -283,6 +295,6 @@ def tile_hstu_pb_kernel(tc, x, h_attn, Wu, bu, g_norm, Wf, b_out, out):
             if hidden and pair % 2 == 1:
                 uv_grouped = gate_pool.tile([P, GROUP, PACK], BF16, name="uv_grouped", align_bytes=64)
                 nc.vector.tensor_copy(
-                    out=uv_grouped[:].rearrange("p (n i) t -> p n t i", i=4),
-                    in_=planes[g2][:].rearrange("p t (n i) -> p n t i", i=4),
+                    out=uv_grouped[:].rearrange("p (n i) t -> p n t i", i=TOKEN_RUN),
+                    in_=planes[g2][:].rearrange("p t (n i) -> p n t i", i=TOKEN_RUN),
                 )

from contextlib import ExitStack

import concourse.mybir as mybir
from concourse.masks import make_identity

F32 = mybir.dt.float32
BF16 = mybir.dt.bfloat16
U32 = mybir.dt.uint32
U8 = mybir.dt.uint8
FP8X4 = mybir.dt.float8_e4m3fn_x4
ACT = mybir.ActivationFunctionType
ALU = mybir.AluOpType

P = 128
PACK = 4
K = 1024
PASSES = K // (P * PACK)
TOKENS = 2048
OUT_DIM = 1024
GROUP = 512
TILES = GROUP // P
CHUNKS = TOKENS // GROUP
HALVES = OUT_DIM // GROUP
TOKEN_TILES = TOKENS // P
HIDDEN_TILES = K // P
PAIRS = HIDDEN_TILES // 2
ROUNDS = CHUNKS * PAIRS
WEIGHT_BLOCKS = PASSES + HALVES
WEIGHT_PAIRS = 2 * WEIGHT_BLOCKS
X_TURN = 6
X_PACK = 5
H_SQUARE = 6
H_SCALE = 5
W_AHEAD = 4
WARM_UP = 6
LAG = 6
TOKEN_RUN = 4
RMS_EPS = 1.1920928955078125e-07

FLOPS = 2 * TOKENS * K * K + 2 * TOKENS * K * OUT_DIM


def within(index, count):
    return 0 <= index < count


def tile_hstu_pb_kernel(tc, x, h_attn, Wu, bu, g_norm, Wf, b_out, out):
    nc = tc.nc

    x_rows = x.flatten_outer_dims().rearrange("(c p i) k -> c i p k", p=P, i=TILES)
    h_rows = h_attn.flatten_outer_dims().rearrange("(c p i) k -> c i p k", p=P, i=TILES)
    out_rows = out.flatten_outer_dims().rearrange("(c p i) o -> c i p o", p=P, i=TILES)
    wu_rows = Wu.rearrange("(g u p e) k -> g u p (e k)", g=PASSES, u=2, p=P, e=2)
    wf_rows = Wf.rearrange("(h v b p) k -> h v p b k", h=HALVES, v=2, b=2, p=P)

    with ExitStack() as stack:

        def open_pool(name, bufs):
            return stack.enter_context(tc.tile_pool(name=name, bufs=bufs))

        keep = open_pool("keep", 1)
        grouped_pool = open_pool("grouped", 8)
        x_pool = open_pool("xcodes", 2)
        norm_pool = open_pool("norm", 2)
        stats_pool = open_pool("stats", 6)
        silu_pool = open_pool("silu", 4)
        gate_pool = open_pool("gate", 2)
        result_pool = open_pool("result", 3)
        psum = stack.enter_context(tc.psum_pool(name="psum", bufs=4))
        stack.enter_context(tc.manual_schedule())

        ident = keep.tile([P, P], F32)
        make_identity(nc, ident[:])
        minus_half = keep.tile([P, 1], F32)
        nc.gpsimd.memset(minus_half[:], -0.5)
        bu_sb = keep.tile([P, HIDDEN_TILES], BF16)
        nc.scalar.dma_start(
            out=bu_sb[:].rearrange("p (q e) -> p q e", e=2), in_=bu.rearrange("(q p e) -> p q e", p=P, e=2)
        )
        g_sb = keep.tile([P, HIDDEN_TILES], BF16)
        nc.scalar.dma_start(
            out=g_sb[:].rearrange("p (q e) -> p q e", e=2), in_=g_norm.rearrange("(q p e) -> p q e", p=P, e=2)
        )
        table_warm = keep.tile([P, 1], F32)
        nc.scalar.activation(out=table_warm[:], in_=minus_half[:], func=ACT.Silu)

        x_sb = [keep.tile([P, TILES * K], BF16, name="x%d" % c) for c in range(CHUNKS)]
        h_sb = [keep.tile([P, TILES * K], BF16, name="h%d" % c) for c in range(CHUNKS)]
        w_sb = [keep.tile([P, TILES * K], BF16, name="w%d" % block) for block in range(WEIGHT_BLOCKS)]
        b_out_sb = keep.tile([P, OUT_DIM], BF16)

        def tile_of(rows, i):
            return rows[:, i * K : (i + 1) * K]

        for r in range(-WARM_UP, ROUNDS):
            if within(r + H_SQUARE, TOKEN_TILES):
                c, i = divmod(r + H_SQUARE, TILES)
                nc.sync.dma_start(out=tile_of(h_sb[c], i), in_=h_rows[c][i])
            if within(r + X_TURN, TOKEN_TILES):
                c, i = divmod(r + X_TURN, TILES)
                nc.sync.dma_start(out=tile_of(x_sb[c], i), in_=x_rows[c][i])
            if within(r + W_AHEAD, WEIGHT_PAIRS):
                block, v = divmod(r + W_AHEAD, 2)
                both = w_sb[block][:, 2 * v * K : (2 * v + 2) * K]
                if block < PASSES:
                    nc.sync.dma_start(out=both, in_=wu_rows[block][v])
                else:
                    nc.sync.dma_start(out=both.rearrange("p (b k) -> p b k", b=2), in_=wf_rows[block - PASSES][v])
            if r + W_AHEAD == WEIGHT_PAIRS:
                nc.sync.dma_start(out=b_out_sb[:], in_=b_out.partition_broadcast(P))

        def codes_and_scales(pool, name):
            codes = pool.tile([P, PASSES * GROUP], U32, name=name + "_codes", align_bytes=64)
            scales = pool.tile([P, PASSES * GROUP], U8, name=name + "_scales", align_bytes=64)
            return codes, scales

        def turn(rows, b, ring):
            words = rows[:].bitcast(F32)
            turned = psum.tile([P, PASSES, 2, P], F32, name="turned", tag=ring)
            for g in range(PASSES):
                for u in range(2):
                    first = b * (K // 2) + (2 * g + u) * P
                    nc.tensor.transpose(turned[:, g, u, :], words[:, first : first + P], ident[:])
            return turned

        def spread(copy, turned):
            grouped = grouped_pool.tile([P, PASSES * P * PACK], BF16, name="grouped", align_bytes=64)
            copy(
                out=grouped[:].bitcast(F32).rearrange("p (g r u) -> p g r u", g=PASSES, u=2),
                in_=turned[:].rearrange("p g u r -> p g r u"),
            )
            return grouped

        def pack(grouped, operand, b):
            codes, scales = operand
            for g in range(PASSES):
                cols = slice(g * GROUP + b * P, g * GROUP + (b + 1) * P)
                nc.vector.quantize_mx(
                    out=codes[:, cols].bitcast(FP8X4),
                    scales=scales[:, cols],
                    in_=grouped[:, g * P * PACK : (g + 1) * P * PACK],
                )

        def mx_product(stationary, m_tile, moving):
            bank = psum.tile([P, GROUP], F32, name="acc", tag="mx")
            for g in range(PASSES):
                m_cols = slice(g * GROUP + m_tile * P, g * GROUP + (m_tile + 1) * P)
                n_cols = slice(g * GROUP, (g + 1) * GROUP)
                nc.tensor.matmul_mx(
                    out=bank[:],
                    lhsT=stationary[0][:, m_cols].bitcast(FP8X4),
                    lhsT_scale=stationary[1][:, m_cols],
                    rhs=moving[0][:, n_cols].bitcast(FP8X4),
                    rhs_scale=moving[1][:, n_cols],
                    start=(g == 0),
                    stop=(g == PASSES - 1),
                )
            return bank

        def inverse_rms(t):
            squares = norm_pool.tile([P, K], BF16, name="squares")
            mean_sq = stats_pool.tile([P, 1], F32, name="mean_sq")
            nc.scalar.activation(
                out=squares[:],
                in_=tile_of(h_sb[t // TILES], t % TILES),
                func=ACT.Square,
                scale=K**-0.5,
                accum_out=mean_sq[:],
            )
            shifted = stats_pool.tile([P, 1], F32, name="shifted")
            nc.gpsimd.tensor_scalar(
                out=shifted[:], in0=mean_sq[:], scalar1=1.0, scalar2=RMS_EPS, op0=ALU.mult, op1=ALU.add
            )
            rstd = stats_pool.tile([P, 1], F32, name="rstd")
            nc.gpsimd.tensor_tensor(out=rstd[:], in0=shifted[:], in1=minus_half[:], op=ALU.pow)
            return rstd

        def sorted_half(t, half):
            q_range = slice(half * PAIRS // 2, (half + 1) * PAIRS // 2)
            sorted_out = h_norm_of[t // TILES][:, t % TILES, :].rearrange("p (q e m) -> p q e m", e=2, m=P)
            sorted_in = tile_of(h_sb[t // TILES], t % TILES).rearrange("p (q m e) -> p q e m", m=P, e=2)
            return sorted_out[:, q_range], sorted_in[:, q_range]

        def normalise(engine, t, half):
            sorted_out, sorted_in = sorted_half(t, half)
            engine.tensor_scalar(
                out=sorted_out, in0=sorted_in, scalar1=rstd_of[t][:], scalar2=0.0, op0=ALU.mult, op1=ALU.add
            )

        def normalise_on_scalar(t, half):
            sorted_out, sorted_in = sorted_half(t, half)
            nc.scalar.activation(out=sorted_out, in_=sorted_in, func=ACT.Copy, scale=rstd_of[t][:])

        w_q = [codes_and_scales(keep, "w%d" % block) for block in range(WEIGHT_BLOCKS)]
        x_q = {}
        uv_q = {}
        h_norm_of = {}
        planes = {}
        x_grouped = {}
        rstd_of = {}

        for r in range(-WARM_UP, ROUNDS + LAG):
            chunk, pair = divmod(r, PAIRS)
            hidden = [2 * pair, 2 * pair + 1] if within(r, ROUNDS) else []
            g2 = pair // 2
            behind = r - LAG
            x_new = r + X_TURN
            x_ready = r + X_PACK
            h_new = r + H_SQUARE
            h_ready = r + H_SCALE
            w_new = r + W_AHEAD
            early = x_new < TILES

            z = [mx_product(w_q[g2], j % PACK, x_q[chunk]) for j in hidden]
            projected = []
            if within(behind, TOKEN_TILES):
                projected = [
                    mx_product(uv_q[behind // TILES], behind % TILES, w_q[PASSES + h]) for h in range(HALVES)
                ]

            h_turned = []
            for j in hidden:
                h_turned.append(psum.tile([P, GROUP], F32, name="h_turned", tag="turn"))
                for i in range(TILES):
                    nc.tensor.transpose(
                        h_turned[-1][:, i * P : (i + 1) * P], h_norm_of[chunk][:, i, j * P : (j + 1) * P], ident[:]
                    )
            if within(x_new, TOKEN_TILES):
                x_turned = turn(x_sb[x_new // TILES], x_new % TILES, "turn")
            w_turned = []
            if within(w_new, WEIGHT_PAIRS):
                w_tiles = [2 * (w_new % 2), 2 * (w_new % 2) + 1]
                w_turned = [turn(w_sb[w_new // 2], b, "mx") for b in w_tiles]

            u = []
            for s, j in enumerate(hidden):
                u.append(silu_pool.tile([P, GROUP], F32, name="u"))
                nc.scalar.activation(out=u[s][:], in_=z[s][:], func=ACT.Silu, bias=bu_sb[:, j : j + 1], scale=1.0)
            if within(h_new, TOKEN_TILES):
                rstd_of[h_new] = inverse_rms(h_new)
            if within(x_new, TOKEN_TILES) and not early:
                x_grouped[x_new] = spread(nc.scalar.copy, x_turned)
            w_grouped = [spread(nc.scalar.copy, w_turned[0])] if w_turned and r < 0 else []

            if within(h_ready, TOKEN_TILES):
                if h_ready % TILES == 0:
                    h_norm_of[h_ready // TILES] = norm_pool.tile([P, TILES, K], F32, name="h_norm")
                if h_ready >= TILES:
                    normalise(nc.gpsimd, h_ready, 0)
                    normalise_on_scalar(h_ready, 1)

            if projected:
                result = result_pool.tile([P, OUT_DIM], F32, name="result")
                for h in range(HALVES):
                    o_cols = slice(h * GROUP, (h + 1) * GROUP)
                    nc.vector.tensor_tensor(
                        out=result[:, o_cols], in0=projected[h][:], in1=b_out_sb[:, o_cols], op=ALU.add
                    )
                    nc.sync.dma_start(out=out_rows[behind // TILES][behind % TILES][:, o_cols], in_=result[:, o_cols])
            if hidden and pair % 2 == 0:
                planes[g2] = gate_pool.tile([P, PACK, GROUP], BF16, name="planes")
            for s, j in enumerate(hidden):
                nc.vector.scalar_tensor_tensor(
                    out=planes[g2][:, j % PACK, :],
                    in0=h_turned[s][:],
                    scalar=g_sb[:, j : j + 1],
                    in1=u[s][:],
                    op0=ALU.mult,
                    op1=ALU.mult,
                )
            if within(x_new, TOKEN_TILES) and early:
                x_grouped[x_new] = spread(nc.vector.tensor_copy, x_turned)
            for turned in w_turned[len(w_grouped) :]:
                w_grouped.append(spread(nc.vector.tensor_copy, turned))
            if within(h_ready, TILES):
                normalise(nc.vector, h_ready, 0)
                normalise(nc.vector, h_ready, 1)
            if within(x_ready, TOKEN_TILES):
                if x_ready % TILES == 0:
                    x_q[x_ready // TILES] = codes_and_scales(x_pool, "x")
                pack(x_grouped[x_ready], x_q[x_ready // TILES], x_ready % TILES)
            for s in range(len(w_turned)):
                pack(w_grouped[s], w_q[w_new // 2], w_tiles[s])
            if within(r - 1, ROUNDS) and pair % 2 == 0:
                done_chunk, done_pair = divmod(r - 1, PAIRS)
                done_pass = done_pair // 2
                if done_pass == 0:
                    uv_q[done_chunk] = codes_and_scales(gate_pool, "uv")
                cols = slice(done_pass * GROUP, (done_pass + 1) * GROUP)
                nc.vector.quantize_mx(
                    out=uv_q[done_chunk][0][:, cols].bitcast(FP8X4),
                    scales=uv_q[done_chunk][1][:, cols],
                    in_=uv_grouped[:].rearrange("p r t -> p (r t)"),
                )
            if hidden and pair % 2 == 1:
                uv_grouped = gate_pool.tile([P, GROUP, PACK], BF16, name="uv_grouped", align_bytes=64)
                nc.vector.tensor_copy(
                    out=uv_grouped[:].rearrange("p (n i) t -> p n t i", i=TOKEN_RUN),
                    in_=planes[g2][:].rearrange("p t (n i) -> p n t i", i=TOKEN_RUN),
                )
